import numpy as np
import ml_dtypes

BF16 = ml_dtypes.bfloat16


def bf(x):
    return np.asarray(x, np.float32).astype(BF16)


def f32(x):
    return np.asarray(x, np.float32)


def f64(x):
    return np.asarray(x).astype(np.float64)


def striped(idx):
    return np.tile(idx.reshape(-1, 16).T, (8, 1))


D, S, M, N = 128, 4096, 128, 2048


def setup_inputs():
    return {"table": bf(np.random.standard_normal((D, S))), "w": bf(np.random.standard_normal((D, M)) / np.sqrt(D)), "b": f32(0.1 * np.random.standard_normal((M, 1))), "offs": striped(np.random.permutation(np.tile(np.arange(S), 2))[:N])}


def reference(table, w, b, offs):
    idx = offs[:16].T.reshape(-1)
    x = f64(table)[:, idx]
    return np.maximum(f64(w).T @ x + f64(b), 0.0) + x

@@ -1,0 +1,47 @@
+import concourse.mybir as mybir
+from concourse.masks import make_identity
+
+D, S, M, N = 128, 4096, 128, 2048
+PIECE = 512
+PIECES = N // PIECE
+COLS = PIECE // 16
+FLOPS = 2 * D * M * N
+
+BF16, F32, U16 = mybir.dt.bfloat16, mybir.dt.float32, mybir.dt.uint16
+RELU = mybir.ActivationFunctionType.Relu
+ADD = mybir.AluOpType.add
+
+
+def tile_scriptwriter_cpre_kernel(tc, table, w, b, offs, out):
+    nc = tc.nc
+    with (
+        tc.tile_pool(name="held", bufs=1) as held,
+        tc.tile_pool(name="work", bufs=PIECES) as work,
+        tc.psum_pool(name="psum", bufs=PIECES) as psum,
+    ):
+        window = held.tile([D, S], BF16, name="window")
+        offsets = held.tile([128, N // 16], U16, name="offsets")
+        weights = held.tile([D, M], BF16, name="weights")
+        bias = held.tile([M, 1], F32, name="bias")
+        identity = held.tile([D, D], BF16, name="identity")
+
+        nc.sync.dma_start(window[:], table)
+        nc.sync.dma_start(offsets[:], offs)
+        nc.scalar.dma_start(weights[:], w)
+        nc.scalar.dma_start(bias[:], b)
+        make_identity(nc, identity[:])
+
+        for p in range(PIECES):
+            picked = window[:].indirect(offsets[:, p * COLS : (p + 1) * COLS])
+
+            projected = psum.tile([M, PIECE], F32, name="projected")
+            nc.tensor.matmul(projected[:], weights[:], picked, start=True, stop=True)
+            residual = psum.tile([D, PIECE], F32, name="residual")
+            nc.tensor.matmul(residual[:], identity[:], picked, start=True, stop=True)
+
+            relu = work.tile([M, PIECE], F32, name="relu")
+            nc.scalar.activation(relu[:], projected[:], RELU, bias=bias[:])
+            result = work.tile([M, PIECE], F32, name="result")
+            nc.vector.tensor_tensor(result[:], relu[:], residual[:], ADD)
+
+            nc.sync.dma_start(out[:, p * PIECE : (p + 1) * PIECE], result[:])

@@ -2,9 +2,13 @@ import concourse.mybir as mybir
 from concourse.masks import make_identity
 
 D, S, M, N = 128, 4096, 128, 2048
-PIECE = 512
-PIECES = N // PIECE
-COLS = PIECE // 16
+BANK = 512
+BANKS = 8
+WIDTHS = (BANK, BANK, BANK, BANK)
+assert sum(WIDTHS) == N
+PIECES = len(WIDTHS)
+STARTS = [sum(WIDTHS[:p]) for p in range(PIECES)]
+LEAD = 1
 FLOPS = 2 * D * M * N
 
 BF16, F32, U16 = mybir.dt.bfloat16, mybir.dt.float32, mybir.dt.uint16
@@ -17,7 +21,7 @@ def tile_scriptwriter_cpre_kernel(tc, table, w, b, offs, out):
     with (
         tc.tile_pool(name="held", bufs=1) as held,
         tc.tile_pool(name="work", bufs=PIECES) as work,
-        tc.psum_pool(name="psum", bufs=PIECES) as psum,
+        tc.psum_pool(name="psum", bufs=BANKS) as psum,
     ):
         window = held.tile([D, S], BF16, name="window")
         offsets = held.tile([128, N // 16], U16, name="offsets")
@@ -31,17 +35,26 @@ def tile_scriptwriter_cpre_kernel(tc, table, w, b, offs, out):
         nc.scalar.dma_start(bias[:], b)
         make_identity(nc, identity[:])
 
-        for p in range(PIECES):
-            picked = window[:].indirect(offsets[:, p * COLS : (p + 1) * COLS])
+        def picked(p):
+            return window[:].indirect(offsets[:, STARTS[p] // 16 : (STARTS[p] + WIDTHS[p]) // 16])
 
-            projected = psum.tile([M, PIECE], F32, name="projected")
-            nc.tensor.matmul(projected[:], weights[:], picked, start=True, stop=True)
-            residual = psum.tile([D, PIECE], F32, name="residual")
-            nc.tensor.matmul(residual[:], identity[:], picked, start=True, stop=True)
-
-            relu = work.tile([M, PIECE], F32, name="relu")
+        def project(p):
+            projected = psum.tile([M, WIDTHS[p]], F32, name="projected", tag="bank")
+            nc.tensor.matmul(projected[:], weights[:], picked(p), start=True, stop=True)
+            relu = work.tile([M, WIDTHS[p]], F32, name="relu")
             nc.scalar.activation(relu[:], projected[:], RELU, bias=bias[:])
-            result = work.tile([M, PIECE], F32, name="result")
-            nc.vector.tensor_tensor(result[:], relu[:], residual[:], ADD)
+            return relu
 
-            nc.sync.dma_start(out[:, p * PIECE : (p + 1) * PIECE], result[:])
+        def finish(p, relu):
+            residual = psum.tile([D, WIDTHS[p]], F32, name="residual", tag="bank")
+            nc.tensor.matmul(residual[:], identity[:], picked(p), start=True, stop=True)
+            result = work.tile([M, WIDTHS[p]], F32, name="result")
+            nc.vector.tensor_tensor(result[:], relu[:], residual[:], ADD)
+            nc.sync.dma_start(out[:, STARTS[p] : STARTS[p] + WIDTHS[p]], result[:])
+
+        relus = []
+        for step in range(PIECES + LEAD):
+            if step < PIECES:
+                relus.append(project(step))
+            if step >= LEAD:
+                finish(step - LEAD, relus[step - LEAD])

@@ -2,13 +2,10 @@ import concourse.mybir as mybir
 from concourse.masks import make_identity
 
 D, S, M, N = 128, 4096, 128, 2048
-BANK = 512
+PIECE = 512
+PIECES = N // PIECE
+COLS = PIECE // 16
 BANKS = 8
-WIDTHS = (BANK, BANK, BANK, BANK)
-assert sum(WIDTHS) == N
-PIECES = len(WIDTHS)
-STARTS = [sum(WIDTHS[:p]) for p in range(PIECES)]
-LEAD = 1
 FLOPS = 2 * D * M * N
 
 BF16, F32, U16 = mybir.dt.bfloat16, mybir.dt.float32, mybir.dt.uint16
@@ -29,32 +26,37 @@ def tile_scriptwriter_cpre_kernel(tc, table, w, b, offs, out):
         bias = held.tile([M, 1], F32, name="bias")
         identity = held.tile([D, D], BF16, name="identity")
 
-        nc.sync.dma_start(window[:], table)
         nc.sync.dma_start(offsets[:], offs)
-        nc.scalar.dma_start(weights[:], w)
-        nc.scalar.dma_start(bias[:], b)
+        nc.sync.dma_start(window[:], table)
+        nc.sync.dma_start(weights[:], w)
+        nc.sync.dma_start(bias[:], b)
         make_identity(nc, identity[:])
 
         def picked(p):
-            return window[:].indirect(offsets[:, STARTS[p] // 16 : (STARTS[p] + WIDTHS[p]) // 16])
+            return window[:].indirect(offsets[:, p * COLS : (p + 1) * COLS])
+
+        def pick(p):
+            residual = psum.tile([D, PIECE], F32, name="residual", tag="bank")
+            nc.tensor.matmul(residual[:], identity[:], picked(p), start=True, stop=True)
+            return residual
 
         def project(p):
-            projected = psum.tile([M, WIDTHS[p]], F32, name="projected", tag="bank")
+            projected = psum.tile([M, PIECE], F32, name="projected", tag="bank")
             nc.tensor.matmul(projected[:], weights[:], picked(p), start=True, stop=True)
-            relu = work.tile([M, WIDTHS[p]], F32, name="relu")
+            relu = work.tile([M, PIECE], F32, name="relu")
             nc.scalar.activation(relu[:], projected[:], RELU, bias=bias[:])
             return relu
 
-        def finish(p, relu):
-            residual = psum.tile([D, WIDTHS[p]], F32, name="residual", tag="bank")
-            nc.tensor.matmul(residual[:], identity[:], picked(p), start=True, stop=True)
-            result = work.tile([M, WIDTHS[p]], F32, name="result")
+        def finish(p, relu, residual):
+            result = work.tile([M, PIECE], F32, name="result")
             nc.vector.tensor_tensor(result[:], relu[:], residual[:], ADD)
-            nc.sync.dma_start(out[:, STARTS[p] : STARTS[p] + WIDTHS[p]], result[:])
+            nc.sync.dma_start(out[:, p * PIECE : (p + 1) * PIECE], result[:])
 
-        relus = []
-        for step in range(PIECES + LEAD):
-            if step < PIECES:
-                relus.append(project(step))
-            if step >= LEAD:
-                finish(step - LEAD, relus[step - LEAD])
+        residual = pick(0)
+        relu = project(0)
+        for p in range(PIECES):
+            following = project(p + 1) if p + 1 < PIECES else None
+            if p > 0:
+                residual = pick(p)
+            finish(p, relu, residual)
+            relu = following

@@ -52,11 +52,28 @@ def tile_scriptwriter_cpre_kernel(tc, table, w, b, offs, out):
             nc.vector.tensor_tensor(result[:], relu[:], residual[:], ADD)
             nc.sync.dma_start(out[:, p * PIECE : (p + 1) * PIECE], result[:])
 
+        def finish_last(relu):
+            result = work.tile([M, PIECE], F32, name="result")
+            for half in range(2):
+                first = (PIECES - 1) * COLS + half * COLS // 2
+                residual = psum.tile([D, PIECE // 2], F32, name="residual", tag="bank")
+                nc.tensor.matmul(
+                    residual[:],
+                    identity[:],
+                    window[:].indirect(offsets[:, first : first + COLS // 2]),
+                    start=True,
+                    stop=True,
+                )
+                columns = slice(half * PIECE // 2, (half + 1) * PIECE // 2)
+                nc.vector.tensor_tensor(result[:, columns], relu[:, columns], residual[:], ADD)
+            nc.sync.dma_start(out[:, (PIECES - 1) * PIECE :], result[:])
+
         residual = pick(0)
         relu = project(0)
-        for p in range(PIECES):
-            following = project(p + 1) if p + 1 < PIECES else None
+        for p in range(PIECES - 1):
+            following = project(p + 1)
             if p > 0:
                 residual = pick(p)
             finish(p, relu, residual)
             relu = following
+        finish_last(relu)

@@ -4,7 +4,6 @@ from concourse.masks import make_identity
 D, S, M, N = 128, 4096, 128, 2048
 PIECE = 512
 PIECES = N // PIECE
-COLS = PIECE // 16
 BANKS = 8
 FLOPS = 2 * D * M * N
 
@@ -32,48 +31,48 @@ def tile_scriptwriter_cpre_kernel(tc, table, w, b, offs, out):
         nc.sync.dma_start(bias[:], b)
         make_identity(nc, identity[:])
 
-        def picked(p):
-            return window[:].indirect(offsets[:, p * COLS : (p + 1) * COLS])
+        def picked(first, width):
+            return window[:].indirect(offsets[:, first // 16 : (first + width) // 16])
 
-        def pick(p):
-            residual = psum.tile([D, PIECE], F32, name="residual", tag="bank")
-            nc.tensor.matmul(residual[:], identity[:], picked(p), start=True, stop=True)
+        def pick(first, width):
+            residual = psum.tile([D, width], F32, name="residual", tag="bank")
+            nc.tensor.matmul(residual[:], identity[:], picked(first, width), start=True, stop=True)
             return residual
 
-        def project(p):
-            projected = psum.tile([M, PIECE], F32, name="projected", tag="bank")
-            nc.tensor.matmul(projected[:], weights[:], picked(p), start=True, stop=True)
-            relu = work.tile([M, PIECE], F32, name="relu")
-            nc.scalar.activation(relu[:], projected[:], RELU, bias=bias[:])
-            return relu
+        def project(first, width, relu):
+            projected = psum.tile([M, width], F32, name="projected", tag="bank")
+            nc.tensor.matmul(projected[:], weights[:], picked(first, width), start=True, stop=True)
+            nc.scalar.activation(relu, projected[:], RELU, bias=bias[:])
 
-        def finish(p, relu, residual):
-            result = work.tile([M, PIECE], F32, name="result")
-            nc.vector.tensor_tensor(result[:], relu[:], residual[:], ADD)
+        def store(p, result):
             nc.sync.dma_start(out[:, p * PIECE : (p + 1) * PIECE], result[:])
 
-        def finish_last(relu):
-            result = work.tile([M, PIECE], F32, name="result")
-            for half in range(2):
-                first = (PIECES - 1) * COLS + half * COLS // 2
-                residual = psum.tile([D, PIECE // 2], F32, name="residual", tag="bank")
-                nc.tensor.matmul(
-                    residual[:],
-                    identity[:],
-                    window[:].indirect(offsets[:, first : first + COLS // 2]),
-                    start=True,
-                    stop=True,
-                )
-                columns = slice(half * PIECE // 2, (half + 1) * PIECE // 2)
-                nc.vector.tensor_tensor(result[:, columns], relu[:, columns], residual[:], ADD)
-            nc.sync.dma_start(out[:, (PIECES - 1) * PIECE :], result[:])
+        def new_relu():
+            relu = work.tile([M, PIECE], F32, name="relu")
+            return relu
 
-        residual = pick(0)
-        relu = project(0)
-        for p in range(PIECES - 1):
-            following = project(p + 1)
-            if p > 0:
-                residual = pick(p)
-            finish(p, relu, residual)
-            relu = following
-        finish_last(relu)
+        def new_result():
+            result = work.tile([M, PIECE], F32, name="result")
+            return result
+
+        relus = [new_relu() for p in range(PIECES)]
+        results = [new_result() for p in range(PIECES)]
+
+        residual = pick(0, PIECE)
+        project(0, PIECE, relus[0][:])
+        nc.vector.tensor_tensor(results[0][:], relus[0][:], residual[:], ADD)
+        store(0, results[0])
+        for p in range(1, PIECES - 1):
+            project(p * PIECE, PIECE, relus[p][:])
+            residual = pick(p * PIECE, PIECE)
+            nc.vector.tensor_tensor(results[p][:], relus[p][:], residual[:], ADD)
+            store(p, results[p])
+
+        last, half = PIECES - 1, PIECE // 2
+        halves = [slice(0, half), slice(half, PIECE)]
+        for columns in halves:
+            project(last * PIECE + columns.start, half, relus[last][:, columns])
+        for columns in halves:
+            residual = pick(last * PIECE + columns.start, half)
+            nc.vector.tensor_tensor(results[last][:, columns], relus[last][:, columns], residual[:], ADD)
+        store(last, results[last])

@@ -31,6 +31,10 @@ def tile_scriptwriter_cpre_kernel(tc, table, w, b, offs, out):
         nc.sync.dma_start(bias[:], b)
         make_identity(nc, identity[:])
 
+        zero = held.tile([M, 1], F32, name="zero")
+        nc.vector.memset(zero[:], 0.0)
+        nc.scalar.activation(zero[:], zero[:], RELU)
+
         def picked(first, width):
             return window[:].indirect(offsets[:, first // 16 : (first + width) // 16])
 

@@ -2,8 +2,6 @@ import concourse.mybir as mybir
 from concourse.masks import make_identity
 
 D, S, M, N = 128, 4096, 128, 2048
-PIECE = 512
-PIECES = N // PIECE
 BANKS = 8
 FLOPS = 2 * D * M * N
 
@@ -16,7 +14,6 @@ def tile_scriptwriter_cpre_kernel(tc, table, w, b, offs, out):
     nc = tc.nc
     with (
         tc.tile_pool(name="held", bufs=1) as held,
-        tc.tile_pool(name="work", bufs=PIECES) as work,
         tc.psum_pool(name="psum", bufs=BANKS) as psum,
     ):
         window = held.tile([D, S], BF16, name="window")
@@ -24,6 +21,8 @@ def tile_scriptwriter_cpre_kernel(tc, table, w, b, offs, out):
         weights = held.tile([D, M], BF16, name="weights")
         bias = held.tile([M, 1], F32, name="bias")
         identity = held.tile([D, D], BF16, name="identity")
+        relu = held.tile([M, N], F32, name="relu")
+        result = held.tile([M, N], F32, name="result")
 
         nc.sync.dma_start(offsets[:], offs)
         nc.sync.dma_start(window[:], table)
@@ -35,48 +34,36 @@ def tile_scriptwriter_cpre_kernel(tc, table, w, b, offs, out):
         nc.vector.memset(zero[:], 0.0)
         nc.scalar.activation(zero[:], zero[:], RELU)
 
-        def picked(first, width):
-            return window[:].indirect(offsets[:, first // 16 : (first + width) // 16])
+        def picked(run):
+            return window[:].indirect(offsets[:, run.start // 16 : run.stop // 16])
 
-        def pick(first, width):
-            residual = psum.tile([D, width], F32, name="residual", tag="bank")
-            nc.tensor.matmul(residual[:], identity[:], picked(first, width), start=True, stop=True)
+        def project(run):
+            projected = psum.tile([M, run.stop - run.start], F32, name="projected", tag="bank")
+            nc.tensor.matmul(projected[:], weights[:], picked(run), start=True, stop=True)
+            nc.scalar.activation(relu[:, run], projected[:], RELU, bias=bias[:])
+
+        def pick(run):
+            residual = psum.tile([D, run.stop - run.start], F32, name="residual", tag="bank")
+            nc.tensor.matmul(residual[:], identity[:], picked(run), start=True, stop=True)
             return residual
 
-        def project(first, width, relu):
-            projected = psum.tile([M, width], F32, name="projected", tag="bank")
-            nc.tensor.matmul(projected[:], weights[:], picked(first, width), start=True, stop=True)
-            nc.scalar.activation(relu, projected[:], RELU, bias=bias[:])
+        def add(run, residual):
+            nc.vector.tensor_tensor(result[:, run], relu[:, run], residual[:], ADD)
 
-        def store(p, result):
-            nc.sync.dma_start(out[:, p * PIECE : (p + 1) * PIECE], result[:])
+        def store(run):
+            nc.sync.dma_start(out[:, run], result[:, run])
 
-        def new_relu():
-            relu = work.tile([M, PIECE], F32, name="relu")
-            return relu
+        pieces = [[512], [512], [320, 320], [192, 192]]
+        runs = []
+        first = 0
+        for widths in pieces:
+            runs.append([slice(first + sum(widths[:i]), first + sum(widths[: i + 1])) for i in range(len(widths))])
+            first += sum(widths)
 
-        def new_result():
-            result = work.tile([M, PIECE], F32, name="result")
-            return result
-
-        relus = [new_relu() for p in range(PIECES)]
-        results = [new_result() for p in range(PIECES)]
-
-        residual = pick(0, PIECE)
-        project(0, PIECE, relus[0][:])
-        nc.vector.tensor_tensor(results[0][:], relus[0][:], residual[:], ADD)
-        store(0, results[0])
-        for p in range(1, PIECES - 1):
-            project(p * PIECE, PIECE, relus[p][:])
-            residual = pick(p * PIECE, PIECE)
-            nc.vector.tensor_tensor(results[p][:], relus[p][:], residual[:], ADD)
-            store(p, results[p])
-
-        last, half = PIECES - 1, PIECE // 2
-        halves = [slice(0, half), slice(half, PIECE)]
-        for columns in halves:
-            project(last * PIECE + columns.start, half, relus[last][:, columns])
-        for columns in halves:
-            residual = pick(last * PIECE + columns.start, half)
-            nc.vector.tensor_tensor(results[last][:, columns], relus[last][:, columns], residual[:], ADD)
-        store(last, results[last])
+        opening = pick(runs[0][0])
+        for piece in runs:
+            for run in piece:
+                project(run)
+            for run in piece:
+                add(run, opening if run is runs[0][0] else pick(run))
+            store(slice(piece[0].start, piece[-1].stop))

import concourse.mybir as mybir
from concourse.masks import make_identity

D, S, M, N = 128, 4096, 128, 2048
BANKS = 8
FLOPS = 2 * D * M * N

BF16, F32, U16 = mybir.dt.bfloat16, mybir.dt.float32, mybir.dt.uint16
RELU = mybir.ActivationFunctionType.Relu
ADD = mybir.AluOpType.add


def tile_scriptwriter_cpre_kernel(tc, table, w, b, offs, out):
    nc = tc.nc
    with (
        tc.tile_pool(name="held", bufs=1) as held,
        tc.psum_pool(name="psum", bufs=BANKS) as psum,
    ):
        window = held.tile([D, S], BF16, name="window")
        offsets = held.tile([128, N // 16], U16, name="offsets")
        weights = held.tile([D, M], BF16, name="weights")
        bias = held.tile([M, 1], F32, name="bias")
        identity = held.tile([D, D], BF16, name="identity")
        relu = held.tile([M, N], F32, name="relu")
        result = held.tile([M, N], F32, name="result")

        nc.sync.dma_start(offsets[:], offs)
        nc.sync.dma_start(window[:], table)
        nc.sync.dma_start(weights[:], w)
        nc.sync.dma_start(bias[:], b)
        make_identity(nc, identity[:])

        zero = held.tile([M, 1], F32, name="zero")
        nc.vector.memset(zero[:], 0.0)
        nc.scalar.activation(zero[:], zero[:], RELU)

        def picked(run):
            return window[:].indirect(offsets[:, run.start // 16 : run.stop // 16])

        def project(run):
            projected = psum.tile([M, run.stop - run.start], F32, name="projected", tag="bank")
            nc.tensor.matmul(projected[:], weights[:], picked(run), start=True, stop=True)
            nc.scalar.activation(relu[:, run], projected[:], RELU, bias=bias[:])

        def pick(run):
            residual = psum.tile([D, run.stop - run.start], F32, name="residual", tag="bank")
            nc.tensor.matmul(residual[:], identity[:], picked(run), start=True, stop=True)
            return residual

        def add(run, residual):
            nc.vector.tensor_tensor(result[:, run], relu[:, run], residual[:], ADD)

        def store(run):
            nc.sync.dma_start(out[:, run], result[:, run])

        pieces = [[512], [512], [320, 320], [192, 192]]
        runs = []
        first = 0
        for widths in pieces:
            runs.append([slice(first + sum(widths[:i]), first + sum(widths[: i + 1])) for i in range(len(widths))])
            first += sum(widths)

        opening = pick(runs[0][0])
        for piece in runs:
            for run in piece:
                project(run)
            for run in piece:
                add(run, opening if run is runs[0][0] else pick(run))
            store(slice(piece[0].start, piece[-1].stop))
